import numpy as np
import ml_dtypes


def mxq(x, axis, fmt="e4m3"):
    dtype, down = {"e4m3": (ml_dtypes.float8_e4m3fn, 7), "e5m2": (ml_dtypes.float8_e5m2, 14)}[fmt]
    v = np.moveaxis(np.asarray(x, np.float32).astype(ml_dtypes.bfloat16).astype(np.float64), axis, -1)
    blocks = v.reshape(v.shape[:-1] + (-1, 32))
    amax = np.abs(blocks).max(-1, keepdims=True)
    byte = np.maximum(np.where(amax > 0, np.frexp(amax)[1] - 1 + 127, 0) - down, 1)
    scale = np.exp2(byte - 127.0)
    codes = (blocks / scale).astype(np.float32).astype(dtype).astype(np.float64)
    return np.moveaxis((codes * scale).reshape(v.shape), -1, axis)


WIDE = False


def mx_kscale(k):
    if not WIDE:
        return np.ones(k)
    levels = np.array([20, -20, 10, -10, 0])
    a = np.random.permutation(np.resize(levels, k // 512 * 4)).reshape(k // 512, 4)
    idx = np.arange(k)
    return np.exp2(a[idx // 512, idx % 128 // 32])


BF16 = ml_dtypes.bfloat16


def bf(x):
    return np.asarray(x, np.float32).astype(BF16)


def f64(x):
    return np.asarray(x).astype(np.float64)


B, S, H, N, L = 2, 1024, 1024, 1024, 3
T = B * S
EPS = 1e-06


def setup_inputs():
    s = mx_kscale(T).reshape(B, S, 1)
    x0 = bf(np.random.standard_normal((B, S, H)))
    conv_w = bf(np.random.standard_normal((L, N, H)) / np.sqrt(H))
    norm_w = bf(1.0 + 0.1 * np.random.standard_normal(N))
    g = bf(np.random.standard_normal((B, S, N)) * np.exp2(np.random.randint(-12, 1, (B, S, 1))) / s)
    y = f64(x0) @ f64(conv_w).sum(axis=0).T / L
    rinv = 1.0 / np.sqrt(np.sum(y * y, axis=-1, keepdims=True) + EPS * H)
    return {"hidden_states": bf(f64(x0) * s), "conv_w": conv_w, "norm_w": norm_w,
            "y": np.asarray(y, np.float32), "rinv": np.asarray(rinv, np.float32), "grad_out": g}


def reference(hidden_states, conv_w, norm_w, y, rinv, grad_out):
    yf = f64(y)
    r = f64(rinv)
    gw = f64(grad_out) * f64(norm_w)
    dot = np.sum(gw * yf, axis=-1, keepdims=True)
    dy = np.sqrt(H) * r * (gw - yf * (r * r * dot))
    dy2 = dy.reshape(T, N)
    x2 = f64(hidden_states).reshape(T, H)
    dw = (mxq(dy2, 0, "e5m2").T @ mxq(x2, 0, "e4m3")) / L
    return np.broadcast_to(dw, (L, N, H)).copy()

@@ -1,0 +1,211 @@
+from contextlib import ExitStack
+
+import concourse.mybir as mybir
+
+F32 = mybir.dt.float32
+BF16 = mybir.dt.bfloat16
+U32 = mybir.dt.uint32
+U8 = mybir.dt.uint8
+E4M3_X4 = mybir.dt.float8_e4m3fn_x4
+E5M2_X4 = mybir.dt.float8_e5m2_x4
+MULT = mybir.AluOpType.mult
+SUBTRACT = mybir.AluOpType.subtract
+COPY = mybir.ActivationFunctionType.Copy
+
+P = 128
+PACK = 4
+K_PASS = P * PACK
+TOKENS = 2048
+PASSES = TOKENS // K_PASS
+CHANNELS = 1024
+HIDDEN = 1024
+LAYERS = 3
+BANK = 512
+HALF = PACK // 2
+STEPS = PASSES * 2
+AHEAD = 2
+RUN = 4
+
+FLOPS = 2 * TOKENS * CHANNELS * HIDDEN
+BYTES = TOKENS * (2 * HIDDEN + 2 * CHANNELS + 4 * CHANNELS + 4) + 2 * CHANNELS + 4 * LAYERS * CHANNELS * HIDDEN
+
+
+def token_rows(matrix, c):
+    return matrix[c * K_PASS : (c + 1) * K_PASS, :].rearrange("(p j) n -> p j n", j=PACK)
+
+
+def by_token(rows):
+    return rows.rearrange("p j (q i) -> p q j i", i=RUN)
+
+
+def by_column(grouped):
+    return grouped.rearrange("p (q i) j -> p q j i", i=RUN)
+
+
+def tile_conv2dlinalgrmsnorm_v_kernel(tc, hidden_states, conv_w, norm_w, y, rinv, grad_out, out):
+    nc = tc.nc
+    x_dram = hidden_states.flatten_outer_dims()
+    g_dram = grad_out.flatten_outer_dims()
+    y_dram = y.flatten_outer_dims()
+    r_dram = rinv.flatten_outer_dims()
+
+    with ExitStack() as pools:
+        keep = pools.enter_context(tc.tile_pool(name="keep", bufs=1))
+        g_pool = pools.enter_context(tc.tile_pool(name="g_pool", bufs=AHEAD + 1))
+        x_pool = pools.enter_context(tc.tile_pool(name="x_pool", bufs=2))
+        row_pool = pools.enter_context(tc.tile_pool(name="row_pool", bufs=3))
+        dy_pool = pools.enter_context(tc.tile_pool(name="dy_pool", bufs=2))
+        nw_psum = pools.enter_context(tc.psum_pool(name="nw_psum", bufs=2))
+        acc_psum = pools.enter_context(tc.psum_pool(name="acc_psum", bufs=6))
+
+        agw = [keep.tile([P, PACK, CHANNELS], F32, name="agw%d" % c) for c in range(PASSES)]
+        y_sb = [keep.tile([P, PACK, CHANNELS], F32, name="y_sb%d" % c) for c in range(PASSES)]
+        x_codes = keep.tile([P, PASSES, HIDDEN], U32, align_bytes=64)
+        x_scales = keep.tile([P, PASSES, HIDDEN], U8, align_bytes=64)
+        nw_row = keep.tile([P, CHANNELS], BF16)
+        nw_all = keep.tile([P, CHANNELS], BF16)
+        ones = keep.tile([P, P], BF16)
+        r_sb = keep.tile([P, PASSES * PACK], F32)
+        a_sb = keep.tile([P, PASSES * PACK], F32)
+        rsq = keep.tile([P, PASSES * PACK], F32)
+        b_sb = keep.tile([P, PASSES * PACK], F32)
+
+        nc.vector.memset(nw_row[:], 0.0)
+        nc.vector.memset(ones[:], 1.0)
+        nc.scalar.dma_start(out=nw_row[0:1, :], in_=norm_w.unsqueeze(0))
+        nc.scalar.dma_start(
+            out=r_sb[:].rearrange("p (c j) -> p c j", j=PACK),
+            in_=r_dram.rearrange("(c p j) o -> p c (j o)", p=P, j=PACK),
+        )
+
+        g_tiles = {}
+        x_tiles = {}
+
+        def load_g_and_y(step):
+            c, h = divmod(step, 2)
+            rows = slice(h * HALF, (h + 1) * HALF)
+            g_half = g_pool.tile([P, HALF, CHANNELS], BF16)
+            nc.sync.dma_start(out=g_half[:], in_=token_rows(g_dram, c)[:, rows, :])
+            nc.sync.dma_start(out=y_sb[c][:, rows, :], in_=token_rows(y_dram, c)[:, rows, :])
+            g_tiles[step] = g_half
+
+        def load_x(c):
+            x_raw = x_pool.tile([P, PACK, HIDDEN], BF16)
+            nc.sync.dma_start(out=x_raw[:], in_=token_rows(x_dram, c))
+            x_tiles[c] = x_raw
+
+        load_g_and_y(0)
+        load_x(0)
+        load_g_and_y(1)
+
+        for half in range(CHANNELS // BANK):
+            cols = slice(half * BANK, (half + 1) * BANK)
+            nw_bank = nw_psum.tile([P, BANK], F32)
+            nc.tensor.matmul(out=nw_bank[:], lhsT=ones[:], rhs=nw_row[:, cols], start=True, stop=True)
+            nc.scalar.copy(out=nw_all[:, cols], in_=nw_bank[:])
+
+        nc.vector.tensor_scalar(out=a_sb[:], in0=r_sb[:], scalar1=32.0, scalar2=None, op0=MULT)
+        nc.vector.tensor_tensor(out=rsq[:], in0=r_sb[:], in1=r_sb[:], op=MULT)
+
+        x_grouped_tiles = {}
+
+        def regroup_x(c):
+            x_grouped = x_pool.tile([P, HIDDEN, PACK], BF16, align_bytes=64)
+            nc.scalar.copy(out=by_column(x_grouped[:]), in_=by_token(x_tiles[c][:]))
+            x_grouped_tiles[c] = x_grouped
+
+        def quantise_x(c):
+            nc.vector.quantize_mx(
+                out=x_codes[:, c, :].bitcast(E4M3_X4),
+                scales=x_scales[:, c, :],
+                in_=x_grouped_tiles[c][:].rearrange("p w j -> p (w j)"),
+            )
+
+        for step in range(STEPS):
+            c, h = divmod(step, 2)
+            if step + AHEAD < STEPS:
+                load_g_and_y(step + AHEAD)
+                if (step + AHEAD) % 2 == 0:
+                    load_x((step + AHEAD) // 2)
+            for jj in range(HALF):
+                j = h * HALF + jj
+                r = c * PACK + j
+                nc.vector.scalar_tensor_tensor(
+                    out=agw[c][:, j, :],
+                    in0=g_tiles[step][:, jj, :],
+                    scalar=a_sb[:, r : r + 1],
+                    in1=nw_all[:],
+                    op0=MULT,
+                    op1=MULT,
+                )
+            for jj in range(HALF):
+                j = h * HALF + jj
+                r = c * PACK + j
+                unused = row_pool.tile([P, CHANNELS], F32, tag="row")
+                nc.vector.scalar_tensor_tensor(
+                    out=unused[:],
+                    in0=agw[c][:, j, :],
+                    scalar=rsq[:, r : r + 1],
+                    in1=y_sb[c][:, j, :],
+                    op0=MULT,
+                    op1=MULT,
+                    accum_out=b_sb[:, r : r + 1],
+                )
+            if h == 1:
+                regroup_x(c)
+            for jj in range(HALF):
+                j = h * HALF + jj
+                r = c * PACK + j
+                nc.scalar.activation(out=y_sb[c][:, j, :], in_=y_sb[c][:, j, :], func=COPY, scale=b_sb[:, r : r + 1])
+            if h == 1 and c >= 1 and c < PASSES - 1:
+                quantise_x(c - 1)
+        quantise_x(PASSES - 2)
+        quantise_x(PASSES - 1)
+
+        blocks = CHANNELS // P
+        dy_tiles = {}
+
+        def subtract(m, c):
+            if c == 0:
+                dy_grouped = dy_pool.tile([P, PASSES, P, PACK], BF16, align_bytes=64)
+                dy_tiles[m] = dy_grouped
+            cols = slice(m * P, (m + 1) * P)
+            nc.vector.tensor_tensor(
+                out=by_column(dy_tiles[m][:, c, :, :]),
+                in0=by_token(agw[c][:, :, cols]),
+                in1=by_token(y_sb[c][:, :, cols]),
+                op=SUBTRACT,
+            )
+
+        def finish(m):
+            dy_codes = dy_pool.tile([P, PASSES, P], U32, align_bytes=64)
+            dy_scales = dy_pool.tile([P, PASSES, P], U8, align_bytes=64)
+            nc.vector.quantize_mx(
+                out=dy_codes[:].rearrange("p c w -> p (c w)").bitcast(E5M2_X4),
+                scales=dy_scales[:].rearrange("p c w -> p (c w)"),
+                in_=dy_tiles[m][:].rearrange("p c w j -> p (c w j)"),
+            )
+            result = row_pool.tile([P, HIDDEN], F32, tag="row")
+            for half in range(HIDDEN // BANK):
+                cols = slice(half * BANK, (half + 1) * BANK)
+                acc = acc_psum.tile([P, BANK], F32)
+                for c in range(PASSES):
+                    nc.tensor.matmul_mx(
+                        out=acc[:],
+                        lhsT=dy_codes[:, c, :].bitcast(E5M2_X4),
+                        lhsT_scale=dy_scales[:, c, :],
+                        rhs=x_codes[:, c, cols].bitcast(E4M3_X4),
+                        rhs_scale=x_scales[:, c, cols],
+                        start=(c == 0),
+                        stop=(c == PASSES - 1),
+                    )
+                nc.scalar.activation(out=result[:, cols], in_=acc[:], func=COPY, scale=1.0 / LAYERS)
+            for layer in range(LAYERS):
+                nc.sync.dma_start(out=out[layer, m * P : (m + 1) * P, :], in_=result[:])
+
+        for m in range(blocks):
+            for c in range(PASSES):
+                subtract(m, c)
+                if c == 0 and m > 0:
+                    finish(m - 1)
+        finish(blocks - 1)

@@ -55,7 +55,7 @@ def tile_conv2dlinalgrmsnorm_v_kernel(tc, hidden_states, conv_w, norm_w, y, rinv
         x_pool = pools.enter_context(tc.tile_pool(name="x_pool", bufs=2))
         row_pool = pools.enter_context(tc.tile_pool(name="row_pool", bufs=3))
         dy_pool = pools.enter_context(tc.tile_pool(name="dy_pool", bufs=2))
-        nw_psum = pools.enter_context(tc.psum_pool(name="nw_psum", bufs=2))
+        nw_psum = pools.enter_context(tc.psum_pool(name="nw_psum", bufs=1))
         acc_psum = pools.enter_context(tc.psum_pool(name="acc_psum", bufs=6))
 
         agw = [keep.tile([P, PACK, CHANNELS], F32, name="agw%d" % c) for c in range(PASSES)]
@@ -63,7 +63,6 @@ def tile_conv2dlinalgrmsnorm_v_kernel(tc, hidden_states, conv_w, norm_w, y, rinv
         x_codes = keep.tile([P, PASSES, HIDDEN], U32, align_bytes=64)
         x_scales = keep.tile([P, PASSES, HIDDEN], U8, align_bytes=64)
         nw_row = keep.tile([P, CHANNELS], BF16)
-        nw_all = keep.tile([P, CHANNELS], BF16)
         ones = keep.tile([P, P], BF16)
         r_sb = keep.tile([P, PASSES * PACK], F32)
         a_sb = keep.tile([P, PASSES * PACK], F32)
@@ -72,8 +71,8 @@ def tile_conv2dlinalgrmsnorm_v_kernel(tc, hidden_states, conv_w, norm_w, y, rinv
 
         nc.vector.memset(nw_row[:], 0.0)
         nc.vector.memset(ones[:], 1.0)
-        nc.scalar.dma_start(out=nw_row[0:1, :], in_=norm_w.unsqueeze(0))
-        nc.scalar.dma_start(
+        nc.sync.dma_start(out=nw_row[0:1, :], in_=norm_w.unsqueeze(0))
+        nc.sync.dma_start(
             out=r_sb[:].rearrange("p (c j) -> p c j", j=PACK),
             in_=r_dram.rearrange("(c p j) o -> p c (j o)", p=P, j=PACK),
         )
@@ -98,11 +97,10 @@ def tile_conv2dlinalgrmsnorm_v_kernel(tc, hidden_states, conv_w, norm_w, y, rinv
         load_x(0)
         load_g_and_y(1)
 
+        nw_all = nw_psum.tile([P, CHANNELS], BF16)
         for half in range(CHANNELS // BANK):
             cols = slice(half * BANK, (half + 1) * BANK)
-            nw_bank = nw_psum.tile([P, BANK], F32)
-            nc.tensor.matmul(out=nw_bank[:], lhsT=ones[:], rhs=nw_row[:, cols], start=True, stop=True)
-            nc.scalar.copy(out=nw_all[:, cols], in_=nw_bank[:])
+            nc.tensor.matmul(out=nw_all[:, cols], lhsT=ones[:], rhs=nw_row[:, cols], start=True, stop=True)
 
         nc.vector.tensor_scalar(out=a_sb[:], in0=r_sb[:], scalar1=32.0, scalar2=None, op0=MULT)
         nc.vector.tensor_tensor(out=rsq[:], in0=r_sb[:], in1=r_sb[:], op=MULT)
@@ -177,35 +175,49 @@ def tile_conv2dlinalgrmsnorm_v_kernel(tc, hidden_states, conv_w, norm_w, y, rinv
                 op=SUBTRACT,
             )
 
-        def finish(m):
-            dy_codes = dy_pool.tile([P, PASSES, P], U32, align_bytes=64)
-            dy_scales = dy_pool.tile([P, PASSES, P], U8, align_bytes=64)
+        code_tiles = {}
+        acc_tiles = {}
+
+        def quantise_and_multiply(m, c):
+            if c == 0:
+                dy_codes = dy_pool.tile([P, PASSES, P], U32, align_bytes=64)
+                dy_scales = dy_pool.tile([P, PASSES, P], U8, align_bytes=64)
+                code_tiles[m] = (dy_codes, dy_scales)
+            dy_codes, dy_scales = code_tiles[m]
             nc.vector.quantize_mx(
-                out=dy_codes[:].rearrange("p c w -> p (c w)").bitcast(E5M2_X4),
-                scales=dy_scales[:].rearrange("p c w -> p (c w)"),
-                in_=dy_tiles[m][:].rearrange("p c w j -> p (c w j)"),
+                out=dy_codes[:, c, :].bitcast(E5M2_X4),
+                scales=dy_scales[:, c, :],
+                in_=dy_tiles[m][:, c, :, :].rearrange("p w j -> p (w j)"),
             )
+            for half in range(HIDDEN // BANK):
+                cols = slice(half * BANK, (half + 1) * BANK)
+                if c == 0:
+                    acc = acc_psum.tile([P, BANK], F32)
+                    acc_tiles[(m, half)] = acc
+                nc.tensor.matmul_mx(
+                    out=acc_tiles[(m, half)][:],
+                    lhsT=dy_codes[:, c, :].bitcast(E5M2_X4),
+                    lhsT_scale=dy_scales[:, c, :],
+                    rhs=x_codes[:, c, cols].bitcast(E4M3_X4),
+                    rhs_scale=x_scales[:, c, cols],
+                    start=(c == 0),
+                    stop=(c == PASSES - 1),
+                )
+
+        def store(m):
             result = row_pool.tile([P, HIDDEN], F32, tag="row")
             for half in range(HIDDEN // BANK):
                 cols = slice(half * BANK, (half + 1) * BANK)
-                acc = acc_psum.tile([P, BANK], F32)
-                for c in range(PASSES):
-                    nc.tensor.matmul_mx(
-                        out=acc[:],
-                        lhsT=dy_codes[:, c, :].bitcast(E5M2_X4),
-                        lhsT_scale=dy_scales[:, c, :],
-                        rhs=x_codes[:, c, cols].bitcast(E4M3_X4),
-                        rhs_scale=x_scales[:, c, cols],
-                        start=(c == 0),
-                        stop=(c == PASSES - 1),
-                    )
-                nc.scalar.activation(out=result[:, cols], in_=acc[:], func=COPY, scale=1.0 / LAYERS)
+                nc.scalar.activation(out=result[:, cols], in_=acc_tiles[(m, half)][:], func=COPY, scale=1.0 / LAYERS)
             for layer in range(LAYERS):
                 nc.sync.dma_start(out=out[layer, m * P : (m + 1) * P, :], in_=result[:])
 
-        for m in range(blocks):
-            for c in range(PASSES):
-                subtract(m, c)
-                if c == 0 and m > 0:
-                    finish(m - 1)
-        finish(blocks - 1)
+        pieces = [(m, c) for m in range(blocks) for c in range(PASSES)]
+        for index in range(len(pieces) + 1):
+            if index < len(pieces):
+                subtract(*pieces[index])
+            if index > 0:
+                m, c = pieces[index - 1]
+                quantise_and_multiply(m, c)
+                if c == PASSES - 1:
+                    store(m)

@@ -107,16 +107,21 @@ def tile_conv2dlinalgrmsnorm_v_kernel(tc, hidden_states, conv_w, norm_w, y, rinv
 
         x_grouped_tiles = {}
 
-        def regroup_x(c):
-            x_grouped = x_pool.tile([P, HIDDEN, PACK], BF16, align_bytes=64)
-            nc.scalar.copy(out=by_column(x_grouped[:]), in_=by_token(x_tiles[c][:]))
-            x_grouped_tiles[c] = x_grouped
+        def regroup_x(c, half):
+            if half == 0:
+                x_grouped = x_pool.tile([P, BANK, PACK], BF16, align_bytes=64)
+            else:
+                x_grouped = keep.tile([P, BANK, PACK], BF16, align_bytes=64, name="x_late%d" % c)
+            cols = slice(half * BANK, (half + 1) * BANK)
+            nc.scalar.copy(out=by_column(x_grouped[:]), in_=by_token(x_tiles[c][:, :, cols]))
+            x_grouped_tiles[(c, half)] = x_grouped
 
-        def quantise_x(c):
+        def quantise_x(c, half):
+            cols = slice(half * BANK, (half + 1) * BANK)
             nc.vector.quantize_mx(
-                out=x_codes[:, c, :].bitcast(E4M3_X4),
-                scales=x_scales[:, c, :],
-                in_=x_grouped_tiles[c][:].rearrange("p w j -> p (w j)"),
+                out=x_codes[:, c, cols].bitcast(E4M3_X4),
+                scales=x_scales[:, c, cols],
+                in_=x_grouped_tiles[(c, half)][:].rearrange("p w j -> p (w j)"),
             )
 
         for step in range(STEPS):
@@ -149,16 +154,15 @@ def tile_conv2dlinalgrmsnorm_v_kernel(tc, hidden_states, conv_w, norm_w, y, rinv
                     op1=MULT,
                     accum_out=b_sb[:, r : r + 1],
                 )
-            if h == 1:
-                regroup_x(c)
+            regroup_x(c, h)
             for jj in range(HALF):
                 j = h * HALF + jj
                 r = c * PACK + j
                 nc.scalar.activation(out=y_sb[c][:, j, :], in_=y_sb[c][:, j, :], func=COPY, scale=b_sb[:, r : r + 1])
             if h == 1 and c >= 1 and c < PASSES - 1:
-                quantise_x(c - 1)
-        quantise_x(PASSES - 2)
-        quantise_x(PASSES - 1)
+                quantise_x(c - 1, 0)
+        quantise_x(PASSES - 2, 0)
+        quantise_x(PASSES - 1, 0)
 
         blocks = CHANNELS // P
         dy_tiles = {}
@@ -178,7 +182,7 @@ def tile_conv2dlinalgrmsnorm_v_kernel(tc, hidden_states, conv_w, norm_w, y, rinv
         code_tiles = {}
         acc_tiles = {}
 
-        def quantise_and_multiply(m, c):
+        def quantise_dy(m, c):
             if c == 0:
                 dy_codes = dy_pool.tile([P, PASSES, P], U32, align_bytes=64)
                 dy_scales = dy_pool.tile([P, PASSES, P], U8, align_bytes=64)
@@ -189,35 +193,50 @@ def tile_conv2dlinalgrmsnorm_v_kernel(tc, hidden_states, conv_w, norm_w, y, rinv
                 scales=dy_scales[:, c, :],
                 in_=dy_tiles[m][:, c, :, :].rearrange("p w j -> p (w j)"),
             )
-            for half in range(HIDDEN // BANK):
-                cols = slice(half * BANK, (half + 1) * BANK)
-                if c == 0:
-                    acc = acc_psum.tile([P, BANK], F32)
-                    acc_tiles[(m, half)] = acc
-                nc.tensor.matmul_mx(
-                    out=acc_tiles[(m, half)][:],
-                    lhsT=dy_codes[:, c, :].bitcast(E5M2_X4),
-                    lhsT_scale=dy_scales[:, c, :],
-                    rhs=x_codes[:, c, cols].bitcast(E4M3_X4),
-                    rhs_scale=x_scales[:, c, cols],
-                    start=(c == 0),
-                    stop=(c == PASSES - 1),
-                )
 
-        def store(m):
-            result = row_pool.tile([P, HIDDEN], F32, tag="row")
-            for half in range(HIDDEN // BANK):
-                cols = slice(half * BANK, (half + 1) * BANK)
+        def multiply(m, c, half):
+            dy_codes, dy_scales = code_tiles[m]
+            cols = slice(half * BANK, (half + 1) * BANK)
+            if c == 0:
+                acc = acc_psum.tile([P, BANK], F32)
+                acc_tiles[(m, half)] = acc
+            nc.tensor.matmul_mx(
+                out=acc_tiles[(m, half)][:],
+                lhsT=dy_codes[:, c, :].bitcast(E5M2_X4),
+                lhsT_scale=dy_scales[:, c, :],
+                rhs=x_codes[:, c, cols].bitcast(E4M3_X4),
+                rhs_scale=x_scales[:, c, cols],
+                start=(c == 0),
+                stop=(c == PASSES - 1),
+            )
+
+        def store(m, first_half, end_half):
+            result = row_pool.tile([P, (end_half - first_half) * BANK], F32, tag="row")
+            for half in range(first_half, end_half):
+                cols = slice((half - first_half) * BANK, (half - first_half + 1) * BANK)
                 nc.scalar.activation(out=result[:, cols], in_=acc_tiles[(m, half)][:], func=COPY, scale=1.0 / LAYERS)
             for layer in range(LAYERS):
-                nc.sync.dma_start(out=out[layer, m * P : (m + 1) * P, :], in_=result[:])
+                nc.sync.dma_start(
+                    out=out[layer, m * P : (m + 1) * P, first_half * BANK : end_half * BANK], in_=result[:]
+                )
 
+        halves = HIDDEN // BANK
         pieces = [(m, c) for m in range(blocks) for c in range(PASSES)]
         for index in range(len(pieces) + 1):
             if index < len(pieces):
                 subtract(*pieces[index])
             if index > 0:
                 m, c = pieces[index - 1]
-                quantise_and_multiply(m, c)
-                if c == PASSES - 1:
-                    store(m)
+                quantise_dy(m, c)
+                multiply(m, c, 0)
+                if m > 0:
+                    multiply(m, c, 1)
+                    if c == PASSES - 1:
+                        store(m, 0, halves)
+                elif c == PASSES - 1:
+                    store(m, 0, 1)
+                    for late in range(PASSES):
+                        quantise_x(late, 1)
+                    for late in range(PASSES):
+                        multiply(m, late, 1)
+                    store(m, 1, halves)

@@ -215,10 +215,11 @@ def tile_conv2dlinalgrmsnorm_v_kernel(tc, hidden_states, conv_w, norm_w, y, rinv
             for half in range(first_half, end_half):
                 cols = slice((half - first_half) * BANK, (half - first_half + 1) * BANK)
                 nc.scalar.activation(out=result[:, cols], in_=acc_tiles[(m, half)][:], func=COPY, scale=1.0 / LAYERS)
-            for layer in range(LAYERS):
-                nc.sync.dma_start(
-                    out=out[layer, m * P : (m + 1) * P, first_half * BANK : end_half * BANK], in_=result[:]
-                )
+            width = (end_half - first_half) * BANK
+            nc.sync.dma_start(
+                out=out[:, m * P : (m + 1) * P, first_half * BANK : end_half * BANK].rearrange("l p h -> p l h"),
+                in_=result[:].unsqueeze(1).to_broadcast([P, LAYERS, width]),
+            )
 
         halves = HIDDEN // BANK
         pieces = [(m, c) for m in range(blocks) for c in range(PASSES)]

@@ -1,6 +1,7 @@
 from contextlib import ExitStack
 
 import concourse.mybir as mybir
+from concourse.masks import make_identity
 
 F32 = mybir.dt.float32
 BF16 = mybir.dt.bfloat16
@@ -56,7 +57,8 @@ def tile_conv2dlinalgrmsnorm_v_kernel(tc, hidden_states, conv_w, norm_w, y, rinv
         row_pool = pools.enter_context(tc.tile_pool(name="row_pool", bufs=3))
         dy_pool = pools.enter_context(tc.tile_pool(name="dy_pool", bufs=2))
         nw_psum = pools.enter_context(tc.psum_pool(name="nw_psum", bufs=1))
-        acc_psum = pools.enter_context(tc.psum_pool(name="acc_psum", bufs=6))
+        acc_psum = pools.enter_context(tc.psum_pool(name="acc_psum", bufs=5))
+        turn_psum = pools.enter_context(tc.psum_pool(name="turn_psum", bufs=2))
 
         agw = [keep.tile([P, PACK, CHANNELS], F32, name="agw%d" % c) for c in range(PASSES)]
         y_sb = [keep.tile([P, PACK, CHANNELS], F32, name="y_sb%d" % c) for c in range(PASSES)]
@@ -106,6 +108,8 @@ def tile_conv2dlinalgrmsnorm_v_kernel(tc, hidden_states, conv_w, norm_w, y, rinv
         nc.vector.tensor_tensor(out=rsq[:], in0=r_sb[:], in1=r_sb[:], op=MULT)
 
         x_grouped_tiles = {}
+        identity = keep.tile([P, P], BF16)
+        make_identity(nc, identity[:])
 
         def regroup_x(c, half):
             if half == 0:
@@ -113,7 +117,23 @@ def tile_conv2dlinalgrmsnorm_v_kernel(tc, hidden_states, conv_w, norm_w, y, rinv
             else:
                 x_grouped = keep.tile([P, BANK, PACK], BF16, align_bytes=64, name="x_late%d" % c)
             cols = slice(half * BANK, (half + 1) * BANK)
-            nc.scalar.copy(out=by_column(x_grouped[:]), in_=by_token(x_tiles[c][:, :, cols]))
+            if half == 0:
+                nc.scalar.copy(out=by_column(x_grouped[:]), in_=by_token(x_tiles[c][:, :, cols]))
+            else:
+                for bank in range(BANK * PACK // (2 * BANK)):
+                    turned = turn_psum.tile([P, 2 * BANK], BF16)
+                    for part in range(2):
+                        first = half * BANK + (2 * bank + part) * P
+                        nc.tensor.matmul(
+                            out=turned[:, part * BANK : (part + 1) * BANK],
+                            lhsT=identity[:],
+                            rhs=x_tiles[c][:, :, first : first + P].rearrange("p j w -> p w j"),
+                            start=True,
+                            stop=True,
+                        )
+                    nc.scalar.copy(
+                        out=x_grouped[:, 2 * bank * P : 2 * (bank + 1) * P, :].rearrange("p w j -> p (w j)"), in_=turned[:]
+                    )
             x_grouped_tiles[(c, half)] = x_grouped
 
         def quantise_x(c, half):

@@ -10,7 +10,7 @@ U8 = mybir.dt.uint8
 E4M3_X4 = mybir.dt.float8_e4m3fn_x4
 E5M2_X4 = mybir.dt.float8_e5m2_x4
 MULT = mybir.AluOpType.mult
-SUBTRACT = mybir.AluOpType.subtract
+ADD = mybir.AluOpType.add
 COPY = mybir.ActivationFunctionType.Copy
 
 P = 128
@@ -105,7 +105,9 @@ def tile_conv2dlinalgrmsnorm_v_kernel(tc, hidden_states, conv_w, norm_w, y, rinv
             nc.tensor.matmul(out=nw_all[:, cols], lhsT=ones[:], rhs=nw_row[:, cols], start=True, stop=True)
 
         nc.vector.tensor_scalar(out=a_sb[:], in0=r_sb[:], scalar1=32.0, scalar2=None, op0=MULT)
-        nc.vector.tensor_tensor(out=rsq[:], in0=r_sb[:], in1=r_sb[:], op=MULT)
+        nc.vector.scalar_tensor_tensor(out=rsq[:], in0=r_sb[:], scalar=-1.0, in1=r_sb[:], op0=MULT, op1=MULT)
+        identity_f32 = keep.tile([P, P], F32)
+        make_identity(nc, identity_f32[:])
 
         x_grouped_tiles = {}
         identity = keep.tile([P, P], BF16)
@@ -121,7 +123,7 @@ def tile_conv2dlinalgrmsnorm_v_kernel(tc, hidden_states, conv_w, norm_w, y, rinv
                 nc.scalar.copy(out=by_column(x_grouped[:]), in_=by_token(x_tiles[c][:, :, cols]))
             else:
                 for bank in range(BANK * PACK // (2 * BANK)):
-                    turned = turn_psum.tile([P, 2 * BANK], BF16)
+                    turned = turn_psum.tile([P, 2 * BANK], BF16, tag="turned")
                     for part in range(2):
                         first = half * BANK + (2 * bank + part) * P
                         nc.tensor.matmul(
@@ -143,6 +145,20 @@ def tile_conv2dlinalgrmsnorm_v_kernel(tc, hidden_states, conv_w, norm_w, y, rinv
                 scales=x_scales[:, c, cols],
                 in_=x_grouped_tiles[(c, half)][:].rearrange("p w j -> p (w j)"),
             )
+
+        first_dy = dy_pool.tile([P, PASSES, P, PACK], BF16, align_bytes=64, tag="dy_grouped")
+        sum_tiles = {}
+
+        def add_on_tensor(m, c):
+            cols = slice(m * P, (m + 1) * P)
+            sums = turn_psum.tile([P, P, PACK], F32, tag="turned")
+            flat = sums[:].rearrange("p w j -> p (w j)")
+            nc.tensor.matmul(out=flat, lhsT=identity_f32[:], rhs=agw[c][:, :, cols].rearrange("p j w -> p w j"), start=True, stop=False)
+            nc.tensor.matmul(out=flat, lhsT=identity_f32[:], rhs=y_sb[c][:, :, cols].rearrange("p j w -> p w j"), start=False, stop=True)
+            sum_tiles[c] = sums
+
+        def round_on_scalar(c):
+            nc.scalar.copy(out=first_dy[:, c, :, :], in_=sum_tiles[c][:])
 
         for step in range(STEPS):
             c, h = divmod(step, 2)
@@ -174,21 +190,32 @@ def tile_conv2dlinalgrmsnorm_v_kernel(tc, hidden_states, conv_w, norm_w, y, rinv
                     op1=MULT,
                     accum_out=b_sb[:, r : r + 1],
                 )
-            regroup_x(c, h)
-            for jj in range(HALF):
-                j = h * HALF + jj
-                r = c * PACK + j
-                nc.scalar.activation(out=y_sb[c][:, j, :], in_=y_sb[c][:, j, :], func=COPY, scale=b_sb[:, r : r + 1])
+            last_step = step == STEPS - 1
+            if not last_step:
+                regroup_x(c, h)
+            for first, end in ((0, P), (P, CHANNELS)) if last_step else ((0, CHANNELS),):
+                for jj in range(HALF):
+                    j = h * HALF + jj
+                    r = c * PACK + j
+                    nc.scalar.activation(
+                        out=y_sb[c][:, j, first:end], in_=y_sb[c][:, j, first:end], func=COPY, scale=b_sb[:, r : r + 1]
+                    )
+            if last_step:
+                regroup_x(c, h)
             if h == 1 and c >= 1 and c < PASSES - 1:
                 quantise_x(c - 1, 0)
+            if h == 1 and c < PASSES - 1:
+                add_on_tensor(0, c)
+            if h == 0 and c >= 1:
+                round_on_scalar(c - 1)
         quantise_x(PASSES - 2, 0)
         quantise_x(PASSES - 1, 0)
 
         blocks = CHANNELS // P
-        dy_tiles = {}
+        dy_tiles = {0: first_dy}
 
         def subtract(m, c):
-            if c == 0:
+            if c == 0 and m > 0:
                 dy_grouped = dy_pool.tile([P, PASSES, P, PACK], BF16, align_bytes=64)
                 dy_tiles[m] = dy_grouped
             cols = slice(m * P, (m + 1) * P)
@@ -196,7 +223,7 @@ def tile_conv2dlinalgrmsnorm_v_kernel(tc, hidden_states, conv_w, norm_w, y, rinv
                 out=by_column(dy_tiles[m][:, c, :, :]),
                 in0=by_token(agw[c][:, :, cols]),
                 in1=by_token(y_sb[c][:, :, cols]),
-                op=SUBTRACT,
+                op=ADD,
             )
 
         code_tiles = {}
@@ -244,7 +271,7 @@ def tile_conv2dlinalgrmsnorm_v_kernel(tc, hidden_states, conv_w, norm_w, y, rinv
         halves = HIDDEN // BANK
         pieces = [(m, c) for m in range(blocks) for c in range(PASSES)]
         for index in range(len(pieces) + 1):
-            if index < len(pieces):
+            if index < len(pieces) and (pieces[index][0] > 0 or pieces[index][1] == PASSES - 1):
                 subtract(*pieces[index])
             if index > 0:
                 m, c = pieces[index - 1]

@@ -59,6 +59,7 @@ def tile_conv2dlinalgrmsnorm_v_kernel(tc, hidden_states, conv_w, norm_w, y, rinv
         nw_psum = pools.enter_context(tc.psum_pool(name="nw_psum", bufs=1))
         acc_psum = pools.enter_context(tc.psum_pool(name="acc_psum", bufs=5))
         turn_psum = pools.enter_context(tc.psum_pool(name="turn_psum", bufs=2))
+        pools.enter_context(tc.manual_schedule(engines={mybir.EngineType.DVE}))
 
         agw = [keep.tile([P, PACK, CHANNELS], F32, name="agw%d" % c) for c in range(PASSES)]
         y_sb = [keep.tile([P, PACK, CHANNELS], F32, name="y_sb%d" % c) for c in range(PASSES)]

@@ -25,6 +25,7 @@ BANK = 512
 HALF = PACK // 2
 STEPS = PASSES * 2
 AHEAD = 2
+HEAD = 2 * P
 RUN = 4
 
 FLOPS = 2 * TOKENS * CHANNELS * HIDDEN
@@ -147,6 +148,12 @@ def tile_conv2dlinalgrmsnorm_v_kernel(tc, hidden_states, conv_w, norm_w, y, rinv
                 in_=x_grouped_tiles[(c, half)][:].rearrange("p w j -> p (w j)"),
             )
 
+        def scale_y(r, first, end):
+            c, j = divmod(r, PACK)
+            nc.scalar.activation(
+                out=y_sb[c][:, j, first:end], in_=y_sb[c][:, j, first:end], func=COPY, scale=b_sb[:, r : r + 1]
+            )
+
         first_dy = dy_pool.tile([P, PASSES, P, PACK], BF16, align_bytes=64, tag="dy_grouped")
         sum_tiles = {}
 
@@ -191,18 +198,9 @@ def tile_conv2dlinalgrmsnorm_v_kernel(tc, hidden_states, conv_w, norm_w, y, rinv
                     op1=MULT,
                     accum_out=b_sb[:, r : r + 1],
                 )
-            last_step = step == STEPS - 1
-            if not last_step:
-                regroup_x(c, h)
-            for first, end in ((0, P), (P, CHANNELS)) if last_step else ((0, CHANNELS),):
-                for jj in range(HALF):
-                    j = h * HALF + jj
-                    r = c * PACK + j
-                    nc.scalar.activation(
-                        out=y_sb[c][:, j, first:end], in_=y_sb[c][:, j, first:end], func=COPY, scale=b_sb[:, r : r + 1]
-                    )
-            if last_step:
-                regroup_x(c, h)
+            regroup_x(c, h)
+            for jj in range(HALF):
+                scale_y(c * PACK + h * HALF + jj, 0, HEAD if c == PASSES - 1 else CHANNELS)
             if h == 1 and c >= 1 and c < PASSES - 1:
                 quantise_x(c - 1, 0)
             if h == 1 and c < PASSES - 1:
@@ -272,7 +270,8 @@ def tile_conv2dlinalgrmsnorm_v_kernel(tc, hidden_states, conv_w, norm_w, y, rinv
         halves = HIDDEN // BANK
         pieces = [(m, c) for m in range(blocks) for c in range(PASSES)]
         for index in range(len(pieces) + 1):
-            if index < len(pieces) and (pieces[index][0] > 0 or pieces[index][1] == PASSES - 1):
+            ahead = index < len(pieces) and (pieces[index][0] > 0 or pieces[index][1] == PASSES - 1)
+            if ahead and pieces[index] != (1, 0):
                 subtract(*pieces[index])
             if index > 0:
                 m, c = pieces[index - 1]
@@ -284,6 +283,9 @@ def tile_conv2dlinalgrmsnorm_v_kernel(tc, hidden_states, conv_w, norm_w, y, rinv
                         store(m, 0, halves)
                 elif c == PASSES - 1:
                     store(m, 0, 1)
+                    for r in range((PASSES - 1) * PACK, PASSES * PACK):
+                        scale_y(r, HEAD, CHANNELS)
+                    subtract(1, 0)
                     for late in range(PASSES):
                         quantise_x(late, 1)
                     for late in range(PASSES):

@@ -200,7 +200,18 @@ def tile_conv2dlinalgrmsnorm_v_kernel(tc, hidden_states, conv_w, norm_w, y, rinv
                 )
             regroup_x(c, h)
             for jj in range(HALF):
-                scale_y(c * PACK + h * HALF + jj, 0, HEAD if c == PASSES - 1 else CHANNELS)
+                r = c * PACK + h * HALF + jj
+                if jj == HALF - 1 and c < PASSES - 1:
+                    nc.gpsimd.tensor_scalar(
+                        out=y_sb[c][:, h * HALF + jj, :],
+                        in0=y_sb[c][:, h * HALF + jj, :],
+                        scalar1=b_sb[:, r : r + 1],
+                        scalar2=0.0,
+                        op0=MULT,
+                        op1=ADD,
+                    )
+                else:
+                    scale_y(r, 0, HEAD if c == PASSES - 1 else CHANNELS)
             if h == 1 and c >= 1 and c < PASSES - 1:
                 quantise_x(c - 1, 0)
             if h == 1 and c < PASSES - 1:

@@ -185,6 +185,8 @@ def tile_conv2dlinalgrmsnorm_v_kernel(tc, hidden_states, conv_w, norm_w, y, rinv
                     op0=MULT,
                     op1=MULT,
                 )
+            if h == 1 and c >= 1 and c < PASSES - 1:
+                quantise_x(c - 1, 0)
             for jj in range(HALF):
                 j = h * HALF + jj
                 r = c * PACK + j
@@ -212,8 +214,6 @@ def tile_conv2dlinalgrmsnorm_v_kernel(tc, hidden_states, conv_w, norm_w, y, rinv
                     )
                 else:
                     scale_y(r, 0, HEAD if c == PASSES - 1 else CHANNELS)
-            if h == 1 and c >= 1 and c < PASSES - 1:
-                quantise_x(c - 1, 0)
             if h == 1 and c < PASSES - 1:
                 add_on_tensor(0, c)
             if h == 0 and c >= 1:

from contextlib import ExitStack

import concourse.mybir as mybir
from concourse.masks import make_identity

F32 = mybir.dt.float32
BF16 = mybir.dt.bfloat16
U32 = mybir.dt.uint32
U8 = mybir.dt.uint8
E4M3_X4 = mybir.dt.float8_e4m3fn_x4
E5M2_X4 = mybir.dt.float8_e5m2_x4
MULT = mybir.AluOpType.mult
ADD = mybir.AluOpType.add
COPY = mybir.ActivationFunctionType.Copy

P = 128
PACK = 4
K_PASS = P * PACK
TOKENS = 2048
PASSES = TOKENS // K_PASS
CHANNELS = 1024
HIDDEN = 1024
LAYERS = 3
BANK = 512
HALF = PACK // 2
STEPS = PASSES * 2
AHEAD = 2
HEAD = 2 * P
RUN = 4

FLOPS = 2 * TOKENS * CHANNELS * HIDDEN
BYTES = TOKENS * (2 * HIDDEN + 2 * CHANNELS + 4 * CHANNELS + 4) + 2 * CHANNELS + 4 * LAYERS * CHANNELS * HIDDEN


def token_rows(matrix, c):
    return matrix[c * K_PASS : (c + 1) * K_PASS, :].rearrange("(p j) n -> p j n", j=PACK)


def by_token(rows):
    return rows.rearrange("p j (q i) -> p q j i", i=RUN)


def by_column(grouped):
    return grouped.rearrange("p (q i) j -> p q j i", i=RUN)


def tile_conv2dlinalgrmsnorm_v_kernel(tc, hidden_states, conv_w, norm_w, y, rinv, grad_out, out):
    nc = tc.nc
    x_dram = hidden_states.flatten_outer_dims()
    g_dram = grad_out.flatten_outer_dims()
    y_dram = y.flatten_outer_dims()
    r_dram = rinv.flatten_outer_dims()

    with ExitStack() as pools:
        keep = pools.enter_context(tc.tile_pool(name="keep", bufs=1))
        g_pool = pools.enter_context(tc.tile_pool(name="g_pool", bufs=AHEAD + 1))
        x_pool = pools.enter_context(tc.tile_pool(name="x_pool", bufs=2))
        row_pool = pools.enter_context(tc.tile_pool(name="row_pool", bufs=3))
        dy_pool = pools.enter_context(tc.tile_pool(name="dy_pool", bufs=2))
        nw_psum = pools.enter_context(tc.psum_pool(name="nw_psum", bufs=1))
        acc_psum = pools.enter_context(tc.psum_pool(name="acc_psum", bufs=5))
        turn_psum = pools.enter_context(tc.psum_pool(name="turn_psum", bufs=2))
        pools.enter_context(tc.manual_schedule(engines={mybir.EngineType.DVE}))

        agw = [keep.tile([P, PACK, CHANNELS], F32, name="agw%d" % c) for c in range(PASSES)]
        y_sb = [keep.tile([P, PACK, CHANNELS], F32, name="y_sb%d" % c) for c in range(PASSES)]
        x_codes = keep.tile([P, PASSES, HIDDEN], U32, align_bytes=64)
        x_scales = keep.tile([P, PASSES, HIDDEN], U8, align_bytes=64)
        nw_row = keep.tile([P, CHANNELS], BF16)
        ones = keep.tile([P, P], BF16)
        r_sb = keep.tile([P, PASSES * PACK], F32)
        a_sb = keep.tile([P, PASSES * PACK], F32)
        rsq = keep.tile([P, PASSES * PACK], F32)
        b_sb = keep.tile([P, PASSES * PACK], F32)

        nc.vector.memset(nw_row[:], 0.0)
        nc.vector.memset(ones[:], 1.0)
        nc.sync.dma_start(out=nw_row[0:1, :], in_=norm_w.unsqueeze(0))
        nc.sync.dma_start(
            out=r_sb[:].rearrange("p (c j) -> p c j", j=PACK),
            in_=r_dram.rearrange("(c p j) o -> p c (j o)", p=P, j=PACK),
        )

        g_tiles = {}
        x_tiles = {}

        def load_g_and_y(step):
            c, h = divmod(step, 2)
            rows = slice(h * HALF, (h + 1) * HALF)
            g_half = g_pool.tile([P, HALF, CHANNELS], BF16)
            nc.sync.dma_start(out=g_half[:], in_=token_rows(g_dram, c)[:, rows, :])
            nc.sync.dma_start(out=y_sb[c][:, rows, :], in_=token_rows(y_dram, c)[:, rows, :])
            g_tiles[step] = g_half

        def load_x(c):
            x_raw = x_pool.tile([P, PACK, HIDDEN], BF16)
            nc.sync.dma_start(out=x_raw[:], in_=token_rows(x_dram, c))
            x_tiles[c] = x_raw

        load_g_and_y(0)
        load_x(0)
        load_g_and_y(1)

        nw_all = nw_psum.tile([P, CHANNELS], BF16)
        for half in range(CHANNELS // BANK):
            cols = slice(half * BANK, (half + 1) * BANK)
            nc.tensor.matmul(out=nw_all[:, cols], lhsT=ones[:], rhs=nw_row[:, cols], start=True, stop=True)

        nc.vector.tensor_scalar(out=a_sb[:], in0=r_sb[:], scalar1=32.0, scalar2=None, op0=MULT)
        nc.vector.scalar_tensor_tensor(out=rsq[:], in0=r_sb[:], scalar=-1.0, in1=r_sb[:], op0=MULT, op1=MULT)
        identity_f32 = keep.tile([P, P], F32)
        make_identity(nc, identity_f32[:])

        x_grouped_tiles = {}
        identity = keep.tile([P, P], BF16)
        make_identity(nc, identity[:])

        def regroup_x(c, half):
            if half == 0:
                x_grouped = x_pool.tile([P, BANK, PACK], BF16, align_bytes=64)
            else:
                x_grouped = keep.tile([P, BANK, PACK], BF16, align_bytes=64, name="x_late%d" % c)
            cols = slice(half * BANK, (half + 1) * BANK)
            if half == 0:
                nc.scalar.copy(out=by_column(x_grouped[:]), in_=by_token(x_tiles[c][:, :, cols]))
            else:
                for bank in range(BANK * PACK // (2 * BANK)):
                    turned = turn_psum.tile([P, 2 * BANK], BF16, tag="turned")
                    for part in range(2):
                        first = half * BANK + (2 * bank + part) * P
                        nc.tensor.matmul(
                            out=turned[:, part * BANK : (part + 1) * BANK],
                            lhsT=identity[:],
                            rhs=x_tiles[c][:, :, first : first + P].rearrange("p j w -> p w j"),
                            start=True,
                            stop=True,
                        )
                    nc.scalar.copy(
                        out=x_grouped[:, 2 * bank * P : 2 * (bank + 1) * P, :].rearrange("p w j -> p (w j)"), in_=turned[:]
                    )
            x_grouped_tiles[(c, half)] = x_grouped

        def quantise_x(c, half):
            cols = slice(half * BANK, (half + 1) * BANK)
            nc.vector.quantize_mx(
                out=x_codes[:, c, cols].bitcast(E4M3_X4),
                scales=x_scales[:, c, cols],
                in_=x_grouped_tiles[(c, half)][:].rearrange("p w j -> p (w j)"),
            )

        def scale_y(r, first, end):
            c, j = divmod(r, PACK)
            nc.scalar.activation(
                out=y_sb[c][:, j, first:end], in_=y_sb[c][:, j, first:end], func=COPY, scale=b_sb[:, r : r + 1]
            )

        first_dy = dy_pool.tile([P, PASSES, P, PACK], BF16, align_bytes=64, tag="dy_grouped")
        sum_tiles = {}

        def add_on_tensor(m, c):
            cols = slice(m * P, (m + 1) * P)
            sums = turn_psum.tile([P, P, PACK], F32, tag="turned")
            flat = sums[:].rearrange("p w j -> p (w j)")
            nc.tensor.matmul(out=flat, lhsT=identity_f32[:], rhs=agw[c][:, :, cols].rearrange("p j w -> p w j"), start=True, stop=False)
            nc.tensor.matmul(out=flat, lhsT=identity_f32[:], rhs=y_sb[c][:, :, cols].rearrange("p j w -> p w j"), start=False, stop=True)
            sum_tiles[c] = sums

        def round_on_scalar(c):
            nc.scalar.copy(out=first_dy[:, c, :, :], in_=sum_tiles[c][:])

        for step in range(STEPS):
            c, h = divmod(step, 2)
            if step + AHEAD < STEPS:
                load_g_and_y(step + AHEAD)
                if (step + AHEAD) % 2 == 0:
                    load_x((step + AHEAD) // 2)
            for jj in range(HALF):
                j = h * HALF + jj
                r = c * PACK + j
                nc.vector.scalar_tensor_tensor(
                    out=agw[c][:, j, :],
                    in0=g_tiles[step][:, jj, :],
                    scalar=a_sb[:, r : r + 1],
                    in1=nw_all[:],
                    op0=MULT,
                    op1=MULT,
                )
            if h == 1 and c >= 1 and c < PASSES - 1:
                quantise_x(c - 1, 0)
            for jj in range(HALF):
                j = h * HALF + jj
                r = c * PACK + j
                unused = row_pool.tile([P, CHANNELS], F32, tag="row")
                nc.vector.scalar_tensor_tensor(
                    out=unused[:],
                    in0=agw[c][:, j, :],
                    scalar=rsq[:, r : r + 1],
                    in1=y_sb[c][:, j, :],
                    op0=MULT,
                    op1=MULT,
                    accum_out=b_sb[:, r : r + 1],
                )
            regroup_x(c, h)
            for jj in range(HALF):
                r = c * PACK + h * HALF + jj
                if jj == HALF - 1 and c < PASSES - 1:
                    nc.gpsimd.tensor_scalar(
                        out=y_sb[c][:, h * HALF + jj, :],
                        in0=y_sb[c][:, h * HALF + jj, :],
                        scalar1=b_sb[:, r : r + 1],
                        scalar2=0.0,
                        op0=MULT,
                        op1=ADD,
                    )
                else:
                    scale_y(r, 0, HEAD if c == PASSES - 1 else CHANNELS)
            if h == 1 and c < PASSES - 1:
                add_on_tensor(0, c)
            if h == 0 and c >= 1:
                round_on_scalar(c - 1)
        quantise_x(PASSES - 2, 0)
        quantise_x(PASSES - 1, 0)

        blocks = CHANNELS // P
        dy_tiles = {0: first_dy}

        def subtract(m, c):
            if c == 0 and m > 0:
                dy_grouped = dy_pool.tile([P, PASSES, P, PACK], BF16, align_bytes=64)
                dy_tiles[m] = dy_grouped
            cols = slice(m * P, (m + 1) * P)
            nc.vector.tensor_tensor(
                out=by_column(dy_tiles[m][:, c, :, :]),
                in0=by_token(agw[c][:, :, cols]),
                in1=by_token(y_sb[c][:, :, cols]),
                op=ADD,
            )

        code_tiles = {}
        acc_tiles = {}

        def quantise_dy(m, c):
            if c == 0:
                dy_codes = dy_pool.tile([P, PASSES, P], U32, align_bytes=64)
                dy_scales = dy_pool.tile([P, PASSES, P], U8, align_bytes=64)
                code_tiles[m] = (dy_codes, dy_scales)
            dy_codes, dy_scales = code_tiles[m]
            nc.vector.quantize_mx(
                out=dy_codes[:, c, :].bitcast(E5M2_X4),
                scales=dy_scales[:, c, :],
                in_=dy_tiles[m][:, c, :, :].rearrange("p w j -> p (w j)"),
            )

        def multiply(m, c, half):
            dy_codes, dy_scales = code_tiles[m]
            cols = slice(half * BANK, (half + 1) * BANK)
            if c == 0:
                acc = acc_psum.tile([P, BANK], F32)
                acc_tiles[(m, half)] = acc
            nc.tensor.matmul_mx(
                out=acc_tiles[(m, half)][:],
                lhsT=dy_codes[:, c, :].bitcast(E5M2_X4),
                lhsT_scale=dy_scales[:, c, :],
                rhs=x_codes[:, c, cols].bitcast(E4M3_X4),
                rhs_scale=x_scales[:, c, cols],
                start=(c == 0),
                stop=(c == PASSES - 1),
            )

        def store(m, first_half, end_half):
            result = row_pool.tile([P, (end_half - first_half) * BANK], F32, tag="row")
            for half in range(first_half, end_half):
                cols = slice((half - first_half) * BANK, (half - first_half + 1) * BANK)
                nc.scalar.activation(out=result[:, cols], in_=acc_tiles[(m, half)][:], func=COPY, scale=1.0 / LAYERS)
            width = (end_half - first_half) * BANK
            nc.sync.dma_start(
                out=out[:, m * P : (m + 1) * P, first_half * BANK : end_half * BANK].rearrange("l p h -> p l h"),
                in_=result[:].unsqueeze(1).to_broadcast([P, LAYERS, width]),
            )

        halves = HIDDEN // BANK
        pieces = [(m, c) for m in range(blocks) for c in range(PASSES)]
        for index in range(len(pieces) + 1):
            ahead = index < len(pieces) and (pieces[index][0] > 0 or pieces[index][1] == PASSES - 1)
            if ahead and pieces[index] != (1, 0):
                subtract(*pieces[index])
            if index > 0:
                m, c = pieces[index - 1]
                quantise_dy(m, c)
                multiply(m, c, 0)
                if m > 0:
                    multiply(m, c, 1)
                    if c == PASSES - 1:
                        store(m, 0, halves)
                elif c == PASSES - 1:
                    store(m, 0, 1)
                    for r in range((PASSES - 1) * PACK, PASSES * PACK):
                        scale_y(r, HEAD, CHANNELS)
                    subtract(1, 0)
                    for late in range(PASSES):
                        quantise_x(late, 1)
                    for late in range(PASSES):
                        multiply(m, late, 1)
                    store(m, 1, halves)
